import numpy as np
import ml_dtypes


def mxq(x, axis, fmt="e4m3"):
    dtype, down = {"e4m3": (ml_dtypes.float8_e4m3fn, 7), "e5m2": (ml_dtypes.float8_e5m2, 14)}[fmt]
    v = np.moveaxis(np.asarray(x, np.float32).astype(ml_dtypes.bfloat16).astype(np.float64), axis, -1)
    blocks = v.reshape(v.shape[:-1] + (-1, 32))
    amax = np.abs(blocks).max(-1, keepdims=True)
    byte = np.maximum(np.where(amax > 0, np.frexp(amax)[1] - 1 + 127, 0) - down, 1)
    scale = np.exp2(byte - 127.0)
    codes = (blocks / scale).astype(np.float32).astype(dtype).astype(np.float64)
    return np.moveaxis((codes * scale).reshape(v.shape), -1, axis)


WIDE = False


def mx_kscale(k):
    if not WIDE:
        return np.ones(k)
    levels = np.array([10, -10, 5, -5, 0])
    if k % 512:
        return np.exp2(np.random.permutation(np.resize(levels, k // 32))).repeat(32)
    a = np.empty((k // 512, 16))
    for p in range(k // 512):
        a[p, :8] = np.random.permutation(np.resize(levels, 8))
        for g in range(8):
            far = levels[np.abs(levels - a[p, g]) >= 10]
            a[p, g + 8] = far[np.random.randint(len(far))]
    return np.exp2(a.ravel()).repeat(32)


BF16 = ml_dtypes.bfloat16


def bf(x):
    return np.asarray(x, np.float32).astype(BF16)


def f64(x):
    return np.asarray(x).astype(np.float64)


B, IN, H, Z, G = 512, 512, 1024, 256, 4


def gate_scales(zx, dx_w):
    return (f64(zx).transpose(1, 0, 2) @ f64(dx_w).transpose(0, 2, 1)).transpose(1, 0, 2)


def setup_inputs():
    s = mx_kscale(B)
    u = mx_kscale(G * H).reshape(G, H)
    src_x0 = bf(np.random.standard_normal((B, IN)))
    zx = bf(np.random.standard_normal((B, G, Z)))
    dx_w = bf(np.random.standard_normal((G, H, Z)) / np.sqrt(Z))
    w_x0 = bf(np.random.standard_normal((G, H, IN)) / np.sqrt(IN))
    g = bf(np.random.standard_normal((B, G, H)) * np.exp2(np.random.randint(-6, 1, (B, 1, 1))) * 4.0
           / s[:, None, None] * u[None, :, :])
    d_x = gate_scales(zx, dx_w)
    return {"src_x": bf(f64(src_x0) * s[:, None]), "zx": zx, "dx_w": dx_w,
            "w_x": bf(f64(w_x0) / u[:, :, None]),
            "d_x": np.asarray(d_x, np.float32), "grad_out": g}


def reference(src_x, zx, dx_w, w_x, d_x, grad_out):
    dwx = (f64(grad_out) * f64(d_x)).reshape(B, G * H)
    dsrc = mxq(dwx, 1, "e5m2") @ mxq(f64(w_x).reshape(G * H, IN), 0, "e4m3")
    dw = mxq(dwx, 0, "e5m2").T @ mxq(f64(src_x), 0, "e4m3")
    return dsrc, dw.reshape(G, H, IN)

@@ -1,0 +1,209 @@
+from contextlib import ExitStack
+
+import concourse.mybir as mybir
+from concourse.masks import make_identity
+
+B, IN, GH = 512, 512, 4096
+FLOPS = 2 * 2 * B * GH * IN
+BYTES = 2 * B * IN + 2 * GH * IN + 4 * B * GH + 2 * B * GH + 4 * B * IN + 4 * GH * IN
+
+F32 = mybir.dt.float32
+BF16 = mybir.dt.bfloat16
+U32 = mybir.dt.uint32
+U8 = mybir.dt.uint8
+E4 = mybir.dt.float8_e4m3fn_x4
+E5 = mybir.dt.float8_e5m2_x4
+
+P = 128
+J = 4
+UNIT = 512
+NU = GH // UNIT
+IA_V_COLS = [0, 0, 64, 64, 64, 64, 128, 320]
+S_IW = []
+W_LEAD = 1
+V_EVAC = [(6, 1), (6, 3), (7, 1), (7, 3)]
+
+
+def tile_metalstmcell_pa_v_kernel(tc, src_x, zx, dx_w, w_x, d_x, grad_out, out_0, out_1):
+    nc = tc.nc
+    g_v = grad_out.rearrange("(p j) g h -> p j (g h)", j=J)
+    dx_v = d_x.rearrange("(p j) g h -> p j (g h)", j=J)
+    w_v = w_x.rearrange("g h i -> (g h) i").rearrange("(u p j) i -> p u (j i)", p=P, j=J)
+    src_v = src_x.rearrange("(p j) i -> p j i", j=J)
+    o0_v = out_0.rearrange("(p j) i -> p j i", j=J)
+    o1_v = out_1.rearrange("g h i -> (g h) i").rearrange("(u r m) i -> m u r i", r=4, m=P)
+
+    with ExitStack() as ctx:
+        keep = ctx.enter_context(tc.tile_pool(name="keep", bufs=1))
+        big = ctx.enter_context(tc.tile_pool(name="big", bufs=6))
+        work = ctx.enter_context(tc.tile_pool(name="work", bufs=2))
+        acc_pool = ctx.enter_context(tc.psum_pool(name="accp", bufs=1))
+        tp_pool = ctx.enter_context(tc.psum_pool(name="tpp", bufs=2))
+        ps_pool = ctx.enter_context(tc.psum_pool(name="psp", bufs=2))
+        ctx.enter_context(tc.manual_schedule())
+
+        g_of, dx_of, w_of = {}, {}, {}
+
+        def load_g(u0, n):
+            g_t = keep.tile([P, J, n * UNIT], BF16, name="g%d" % u0, tag="g%d" % u0)
+            nc.sync.dma_start(out=g_t[:], in_=g_v[:, :, u0 * UNIT:(u0 + n) * UNIT])
+            for k in range(n):
+                g_of[u0 + k] = g_t[:, :, k * UNIT:(k + 1) * UNIT]
+
+        def load_dx(u0):
+            dx_t = big.tile([P, J, 2 * UNIT], F32, name="dx", tag="big")
+            nc.sync.dma_start(out=dx_t[:], in_=dx_v[:, :, u0 * UNIT:(u0 + 2) * UNIT])
+            for k in range(2):
+                dx_of[u0 + k] = dx_t[:, :, k * UNIT:(k + 1) * UNIT]
+
+        def load_dx_unit(dx_t, u):
+            nc.sync.dma_start(out=dx_t[:, u % 2], in_=dx_v[:, :, u * UNIT:(u + 1) * UNIT])
+            dx_of[u] = dx_t[:, u % 2]
+
+        def load_w1(w_t, u):
+            nc.sync.dma_start(out=w_t[:, u % 2, :], in_=w_v[:, u, :])
+            w_of[u] = w_t[:, u % 2, :].rearrange("p (j i) -> p j i", j=J)
+
+        def load_w(u0):
+            w_t = keep.tile([P, 2, J * IN], BF16, name="w%d" % u0, tag="w%d" % u0)
+            nc.sync.dma_start(out=w_t[:], in_=w_v[:, u0:u0 + 2, :])
+            for k in range(2):
+                w_of[u0 + k] = w_t[:, k, :].rearrange("p (j i) -> p j i", j=J)
+
+        src_t = keep.tile([P, J, IN], BF16, name="src", tag="src")
+        for c in range(NU // 2):
+            dx_t = big.tile([P, 2, J, UNIT], F32, name="dx", tag="big")
+            w_t = keep.tile([P, 2, J * IN], BF16, name="w%d" % c, tag="w%d" % c)
+            for u in (2 * c, 2 * c + 1):
+                load_g(u, 1)
+                load_dx_unit(dx_t, u)
+                load_w1(w_t, u)
+                if u == 0:
+                    nc.sync.dma_start(out=src_t[:], in_=src_v)
+
+        ident = keep.tile([P, P], F32, name="ident", tag="ident")
+        make_identity(nc, ident[:])
+
+        acc = [acc_pool.tile([P, IN], F32, name="acc%d" % j, tag="acc%d" % j) for j in range(J)]
+        src_codes = keep.tile([P, IN], U32, name="srcc", tag="srcc", align_bytes=64)
+        src_scales = keep.tile([P, IN], U8, name="srcs", tag="srcs", align_bytes=64)
+
+        dwx, grp_a, grp_b, grp_w = {}, {}, {}, {}
+        cod_a, sca_a, cod_b, sca_b, cod_w, sca_w = {}, {}, {}, {}, {}, {}
+        ps1, o1, tps = {}, {}, {}
+
+        def mul(u):
+            dwx[u] = work.tile([P, J, UNIT], BF16, name="dwx", tag="dwx", bufs=3)
+            nc.vector.tensor_tensor(out=dwx[u][:], in0=g_of[u], in1=dx_of[u], op=mybir.AluOpType.mult)
+
+        def inter_a(u, eng):
+            if u not in grp_a:
+                grp_a[u] = work.tile([P, UNIT, J], BF16, name="grpa", tag="grpa", bufs=2, align_bytes=64)
+            split = UNIT - IA_V_COLS[u]
+            if eng == "s":
+                nc.scalar.copy(out=grp_a[u][:, 0:split, :], in_=dwx[u][:, :, 0:split].rearrange("p j w -> p w j"))
+            elif split < UNIT:
+                nc.vector.tensor_copy(out=grp_a[u][:, split:UNIT, :], in_=dwx[u][:, :, split:UNIT].rearrange("p j w -> p w j"))
+
+        def quant(grp, fmt, tagc, bufs):
+            codes = work.tile([P, UNIT], U32, name="c" + tagc, tag="c" + tagc, bufs=bufs, align_bytes=64)
+            scales = work.tile([P, UNIT], U8, name="s" + tagc, tag="s" + tagc, bufs=bufs, align_bytes=64)
+            nc.vector.quantize_mx(out=codes[:].bitcast(fmt), scales=scales[:], in_=grp[:].rearrange("p w j -> p (w j)"))
+            return codes, scales
+
+        def quant_a(u):
+            cod_a[u], sca_a[u] = quant(grp_a[u], E5, "a", 2)
+
+        def transposes(u):
+            tps[u] = []
+            for h in range(2):
+                tp = tp_pool.tile([P, 2, 2 * P], F32, name="tp", tag="tp")
+                for jj in range(2):
+                    words = dwx[u][:, 2 * h + jj, :].bitcast(F32)
+                    for e in range(2):
+                        nc.tensor.transpose(tp[:, e, jj * P:(jj + 1) * P], words[:, e:UNIT // 2:2], ident[:])
+                tps[u].append(tp)
+
+        def evac_b(u):
+            grp_b[u] = work.tile([P, UNIT, J], BF16, name="grpb", tag="grpb", bufs=2, align_bytes=64)
+            gw = grp_b[u][:].bitcast(F32)
+            for h in range(2):
+                nc.scalar.copy(out=gw[:, h * 2 * P:(h + 1) * 2 * P, :], in_=tps[u][h][:].rearrange("q e r -> q r e"))
+
+        def quant_b(u):
+            cod_b[u], sca_b[u] = quant(grp_b[u], E5, "b", 2)
+
+        def inter_w(u):
+            grp_w[u] = work.tile([P, IN, J], BF16, name="grpw", tag="grpw", bufs=3, align_bytes=64)
+            if u in S_IW:
+                nc.scalar.copy(out=grp_w[u][:], in_=w_of[u].rearrange("p j i -> p i j"))
+            else:
+                nc.vector.tensor_copy(out=grp_w[u][:], in_=w_of[u].rearrange("p j i -> p i j"))
+
+        def quant_w(u):
+            cod_w[u], sca_w[u] = quant(grp_w[u], E4, "w", W_LEAD + 2)
+
+        def mm1(u, r):
+            ps1[(u, r)] = ps_pool.tile([P, IN], F32, name="ps1", tag="ps1")
+            cols = slice(r * P, (r + 1) * P)
+            nc.tensor.matmul_mx(out=ps1[(u, r)][:], lhsT=cod_a[u][:, cols].bitcast(E5), lhsT_scale=sca_a[u][:, cols],
+                                rhs=src_codes[:].bitcast(E4), rhs_scale=src_scales[:], start=True, stop=True)
+
+        def evac1(u, r):
+            if u % 2 == 0 and r == 0:
+                o1[u // 2] = big.tile([P, 8, IN], F32, name="o1", tag="big")
+            k = (u % 2) * 4 + r
+            dst = o1[u // 2][:, k, :]
+            if (u, r) in V_EVAC:
+                nc.vector.tensor_copy(out=dst, in_=ps1[(u, r)][:])
+            else:
+                nc.scalar.copy(out=dst, in_=ps1[(u, r)][:])
+            if r % 2 == 1:
+                nc.sync.dma_start(out=o1_v[:, u, r - 1:r + 1, :], in_=o1[u // 2][:, k - 1:k + 1, :])
+
+        def mm0(u):
+            for j in range(J):
+                cols = slice(j * P, (j + 1) * P)
+                nc.tensor.matmul_mx(out=acc[j][:], lhsT=cod_b[u][:, cols].bitcast(E5), lhsT_scale=sca_b[u][:, cols],
+                                    rhs=cod_w[u][:].bitcast(E4), rhs_scale=sca_w[u][:], start=(u == 0), stop=(u == NU - 1))
+
+        grp_s = work.tile([P, IN, J], BF16, name="grps", tag="grps", bufs=1, align_bytes=64)
+        mul(0)
+        transposes(0)
+        inter_w(0)
+        nc.vector.tensor_copy(out=grp_s[:], in_=src_t[:].rearrange("p j i -> p i j"))
+
+        for s in range(NU + 1):
+            if s + W_LEAD - 1 < NU:
+                quant_w(s + W_LEAD - 1)
+            if s == 0:
+                nc.vector.quantize_mx(out=src_codes[:].bitcast(E4), scales=src_scales[:], in_=grp_s[:].rearrange("p w j -> p (w j)"))
+            if s >= 1:
+                quant_a(s - 1)
+                quant_b(s - 1)
+            if s + 1 < NU:
+                mul(s + 1)
+            if s + W_LEAD < NU:
+                inter_w(s + W_LEAD)
+            if s < NU:
+                evac_b(s)
+                inter_a(s, "s")
+                inter_a(s, "v")
+            if s >= 1:
+                mm1(s - 1, 0)
+                mm1(s - 1, 1)
+                mm0(s - 1)
+                evac1(s - 1, 0)
+                evac1(s - 1, 1)
+                mm1(s - 1, 2)
+                mm1(s - 1, 3)
+                evac1(s - 1, 2)
+                evac1(s - 1, 3)
+            if s + 1 < NU:
+                transposes(s + 1)
+
+        o0 = big.tile([P, J, IN], F32, name="o0", tag="big")
+        for h in range(2):
+            nc.scalar.copy(out=o0[:, 2 * h, :], in_=acc[2 * h][:])
+            nc.vector.tensor_copy(out=o0[:, 2 * h + 1, :], in_=acc[2 * h + 1][:])
+            nc.sync.dma_start(out=o0_v[:, 2 * h:2 * h + 2, :], in_=o0[:, 2 * h:2 * h + 2, :])

@@ -20,8 +20,10 @@ UNIT = 512
 NU = GH // UNIT
 IA_V_COLS = [0, 0, 64, 64, 64, 64, 128, 320]
 S_IW = []
+WIDE_DX = [2, 3]
+S_IS = False
 W_LEAD = 1
-V_EVAC = [(6, 1), (6, 3), (7, 1), (7, 3)]
+V_EVAC = [(6, 2), (6, 3), (7, 1), (7, 3)]
 
 
 def tile_metalstmcell_pa_v_kernel(tc, src_x, zx, dx_w, w_x, d_x, grad_out, out_0, out_1):
@@ -38,8 +40,7 @@ def tile_metalstmcell_pa_v_kernel(tc, src_x, zx, dx_w, w_x, d_x, grad_out, out_0
         big = ctx.enter_context(tc.tile_pool(name="big", bufs=6))
         work = ctx.enter_context(tc.tile_pool(name="work", bufs=2))
         acc_pool = ctx.enter_context(tc.psum_pool(name="accp", bufs=1))
-        tp_pool = ctx.enter_context(tc.psum_pool(name="tpp", bufs=2))
-        ps_pool = ctx.enter_context(tc.psum_pool(name="psp", bufs=2))
+        ps_pool = ctx.enter_context(tc.psum_pool(name="psp", bufs=4))
         ctx.enter_context(tc.manual_schedule())
 
         g_of, dx_of, w_of = {}, {}, {}
@@ -72,14 +73,22 @@ def tile_metalstmcell_pa_v_kernel(tc, src_x, zx, dx_w, w_x, d_x, grad_out, out_0
 
         src_t = keep.tile([P, J, IN], BF16, name="src", tag="src")
         for c in range(NU // 2):
-            dx_t = big.tile([P, 2, J, UNIT], F32, name="dx", tag="big")
-            w_t = keep.tile([P, 2, J * IN], BF16, name="w%d" % c, tag="w%d" % c)
-            for u in (2 * c, 2 * c + 1):
-                load_g(u, 1)
-                load_dx_unit(dx_t, u)
-                load_w1(w_t, u)
-                if u == 0:
-                    nc.sync.dma_start(out=src_t[:], in_=src_v)
+            if c in WIDE_DX:
+                load_g(2 * c, 2)
+                load_dx(2 * c)
+                load_w(2 * c)
+            else:
+                dx_t = big.tile([P, 2, J, UNIT], F32, name="dx", tag="big")
+                w_t = keep.tile([P, 2, J * IN], BF16, name="w%d" % (2 * c), tag="w%d" % (2 * c))
+                for u in (2 * c, 2 * c + 1):
+                    if c == 0:
+                        load_g(u, 1)
+                    elif u == 2 * c:
+                        load_g(u, 2)
+                    load_dx_unit(dx_t, u)
+                    load_w1(w_t, u)
+                    if u == 0:
+                        nc.sync.dma_start(out=src_t[:], in_=src_v)
 
         ident = keep.tile([P, P], F32, name="ident", tag="ident")
         make_identity(nc, ident[:])
@@ -117,7 +126,7 @@ def tile_metalstmcell_pa_v_kernel(tc, src_x, zx, dx_w, w_x, d_x, grad_out, out_0
         def transposes(u):
             tps[u] = []
             for h in range(2):
-                tp = tp_pool.tile([P, 2, 2 * P], F32, name="tp", tag="tp")
+                tp = ps_pool.tile([P, 2, 2 * P], F32, name="tp", tag="ps")
                 for jj in range(2):
                     words = dwx[u][:, 2 * h + jj, :].bitcast(F32)
                     for e in range(2):
@@ -144,7 +153,7 @@ def tile_metalstmcell_pa_v_kernel(tc, src_x, zx, dx_w, w_x, d_x, grad_out, out_0
             cod_w[u], sca_w[u] = quant(grp_w[u], E4, "w", W_LEAD + 2)
 
         def mm1(u, r):
-            ps1[(u, r)] = ps_pool.tile([P, IN], F32, name="ps1", tag="ps1")
+            ps1[(u, r)] = ps_pool.tile([P, IN], F32, name="ps1", tag="ps")
             cols = slice(r * P, (r + 1) * P)
             nc.tensor.matmul_mx(out=ps1[(u, r)][:], lhsT=cod_a[u][:, cols].bitcast(E5), lhsT_scale=sca_a[u][:, cols],
                                 rhs=src_codes[:].bitcast(E4), rhs_scale=src_scales[:], start=True, stop=True)
@@ -171,34 +180,35 @@ def tile_metalstmcell_pa_v_kernel(tc, src_x, zx, dx_w, w_x, d_x, grad_out, out_0
         mul(0)
         transposes(0)
         inter_w(0)
-        nc.vector.tensor_copy(out=grp_s[:], in_=src_t[:].rearrange("p j i -> p i j"))
+        if S_IS:
+            nc.scalar.copy(out=grp_s[:], in_=src_t[:].rearrange("p j i -> p i j"))
+        else:
+            nc.vector.tensor_copy(out=grp_s[:], in_=src_t[:].rearrange("p j i -> p i j"))
 
         for s in range(NU + 1):
-            if s + W_LEAD - 1 < NU:
-                quant_w(s + W_LEAD - 1)
+            if s < NU:
+                quant_w(s)
             if s == 0:
                 nc.vector.quantize_mx(out=src_codes[:].bitcast(E4), scales=src_scales[:], in_=grp_s[:].rearrange("p w j -> p (w j)"))
-            if s >= 1:
+            if 1 <= s < NU:
                 quant_a(s - 1)
                 quant_b(s - 1)
             if s + 1 < NU:
                 mul(s + 1)
-            if s + W_LEAD < NU:
-                inter_w(s + W_LEAD)
+                inter_w(s + 1)
             if s < NU:
                 evac_b(s)
                 inter_a(s, "s")
                 inter_a(s, "v")
+            if s == NU - 1:
+                quant_a(s)
+                quant_b(s)
             if s >= 1:
-                mm1(s - 1, 0)
-                mm1(s - 1, 1)
+                for r in range(4):
+                    mm1(s - 1, r)
                 mm0(s - 1)
-                evac1(s - 1, 0)
-                evac1(s - 1, 1)
-                mm1(s - 1, 2)
-                mm1(s - 1, 3)
-                evac1(s - 1, 2)
-                evac1(s - 1, 3)
+                for r in range(4):
+                    evac1(s - 1, r)
             if s + 1 < NU:
                 transposes(s + 1)
 

@@ -23,6 +23,7 @@ S_IW = []
 WIDE_DX = [2, 3]
 S_IS = False
 W_LEAD = 1
+R = 2
 V_EVAC = [(6, 2), (6, 3), (7, 1), (7, 3)]
 
 
@@ -33,7 +34,7 @@ def tile_metalstmcell_pa_v_kernel(tc, src_x, zx, dx_w, w_x, d_x, grad_out, out_0
     w_v = w_x.rearrange("g h i -> (g h) i").rearrange("(u p j) i -> p u (j i)", p=P, j=J)
     src_v = src_x.rearrange("(p j) i -> p j i", j=J)
     o0_v = out_0.rearrange("(p j) i -> p j i", j=J)
-    o1_v = out_1.rearrange("g h i -> (g h) i").rearrange("(u r m) i -> m u r i", r=4, m=P)
+    o1_v = out_1.rearrange("g h i -> (g h) i").rearrange("(u g m r) i -> m u g r i", u=NU, r=R, m=P)
 
     with ExitStack() as ctx:
         keep = ctx.enter_context(tc.tile_pool(name="keep", bufs=1))
@@ -81,11 +82,20 @@ def tile_metalstmcell_pa_v_kernel(tc, src_x, zx, dx_w, w_x, d_x, grad_out, out_0
                 dx_t = big.tile([P, 2, J, UNIT], F32, name="dx", tag="big")
                 w_t = keep.tile([P, 2, J * IN], BF16, name="w%d" % (2 * c), tag="w%d" % (2 * c))
                 for u in (2 * c, 2 * c + 1):
-                    if c == 0:
+                    if u == 0:
+                        g_t0 = keep.tile([P, J, UNIT], BF16, name="g0", tag="g0")
+                        for hh in range(2):
+                            js = slice(2 * hh, 2 * hh + 2)
+                            nc.sync.dma_start(out=g_t0[:, js, :], in_=g_v[:, js, 0:UNIT])
+                            nc.sync.dma_start(out=dx_t[:, 0, js, :], in_=dx_v[:, js, 0:UNIT])
+                        g_of[0] = g_t0[:]
+                        dx_of[0] = dx_t[:, 0]
+                    elif u == 1:
                         load_g(u, 1)
                     elif u == 2 * c:
                         load_g(u, 2)
-                    load_dx_unit(dx_t, u)
+                    if u > 0:
+                        load_dx_unit(dx_t, u)
                     load_w1(w_t, u)
                     if u == 0:
                         nc.sync.dma_start(out=src_t[:], in_=src_v)
@@ -97,7 +107,7 @@ def tile_metalstmcell_pa_v_kernel(tc, src_x, zx, dx_w, w_x, d_x, grad_out, out_0
         src_codes = keep.tile([P, IN], U32, name="srcc", tag="srcc", align_bytes=64)
         src_scales = keep.tile([P, IN], U8, name="srcs", tag="srcs", align_bytes=64)
 
-        dwx, grp_a, grp_b, grp_w = {}, {}, {}, {}
+        dwx, grp_a, grp_b, grp_w, grp_ab = {}, {}, {}, {}, {}
         cod_a, sca_a, cod_b, sca_b, cod_w, sca_w = {}, {}, {}, {}, {}, {}
         ps1, o1, tps = {}, {}, {}
 
@@ -105,14 +115,24 @@ def tile_metalstmcell_pa_v_kernel(tc, src_x, zx, dx_w, w_x, d_x, grad_out, out_0
             dwx[u] = work.tile([P, J, UNIT], BF16, name="dwx", tag="dwx", bufs=3)
             nc.vector.tensor_tensor(out=dwx[u][:], in0=g_of[u], in1=dx_of[u], op=mybir.AluOpType.mult)
 
+        def mul_half(u, hh):
+            if hh == 0:
+                dwx[u] = work.tile([P, J, UNIT], BF16, name="dwx", tag="dwx", bufs=3)
+            js = slice(2 * hh, 2 * hh + 2)
+            nc.vector.tensor_tensor(out=dwx[u][:, js, :], in0=g_of[u][:, js, :], in1=dx_of[u][:, js, :], op=mybir.AluOpType.mult)
+
         def inter_a(u, eng):
             if u not in grp_a:
-                grp_a[u] = work.tile([P, UNIT, J], BF16, name="grpa", tag="grpa", bufs=2, align_bytes=64)
-            split = UNIT - IA_V_COLS[u]
+                grp_ab[u] = work.tile([P, 2, UNIT, J], BF16, name="grpab", tag="grpab", bufs=2, align_bytes=64)
+                grp_a[u] = grp_ab[u][:, 0]
+                grp_b[u] = grp_ab[u][:, 1]
+            ms = (UNIT - IA_V_COLS[u]) // R
+            dst = grp_a[u].rearrange("p (r m) j -> p r m j", r=R)
+            srcv = dwx[u][:].rearrange("p j (m r) -> p r m j", r=R)
             if eng == "s":
-                nc.scalar.copy(out=grp_a[u][:, 0:split, :], in_=dwx[u][:, :, 0:split].rearrange("p j w -> p w j"))
-            elif split < UNIT:
-                nc.vector.tensor_copy(out=grp_a[u][:, split:UNIT, :], in_=dwx[u][:, :, split:UNIT].rearrange("p j w -> p w j"))
+                nc.scalar.copy(out=dst[:, :, 0:ms, :], in_=srcv[:, :, 0:ms, :])
+            elif ms < UNIT // R:
+                nc.vector.tensor_copy(out=dst[:, :, ms:UNIT // R, :], in_=srcv[:, :, ms:UNIT // R, :])
 
         def quant(grp, fmt, tagc, bufs):
             codes = work.tile([P, UNIT], U32, name="c" + tagc, tag="c" + tagc, bufs=bufs, align_bytes=64)
@@ -120,12 +140,17 @@ def tile_metalstmcell_pa_v_kernel(tc, src_x, zx, dx_w, w_x, d_x, grad_out, out_0
             nc.vector.quantize_mx(out=codes[:].bitcast(fmt), scales=scales[:], in_=grp[:].rearrange("p w j -> p (w j)"))
             return codes, scales
 
-        def quant_a(u):
-            cod_a[u], sca_a[u] = quant(grp_a[u], E5, "a", 2)
+        def quant_ab(u):
+            codes = work.tile([P, 2 * UNIT], U32, name="cab", tag="cab", bufs=2, align_bytes=64)
+            scales = work.tile([P, 2 * UNIT], U8, name="sab", tag="sab", bufs=2, align_bytes=64)
+            nc.vector.quantize_mx(out=codes[:].bitcast(E5), scales=scales[:], in_=grp_ab[u][:].rearrange("p a w j -> p (a w j)"))
+            cod_a[u], sca_a[u] = codes[:, 0:UNIT], scales[:, 0:UNIT]
+            cod_b[u], sca_b[u] = codes[:, UNIT:2 * UNIT], scales[:, UNIT:2 * UNIT]
 
-        def transposes(u):
-            tps[u] = []
-            for h in range(2):
+        def transposes(u, banks=(0, 1)):
+            if u not in tps:
+                tps[u] = []
+            for h in banks:
                 tp = ps_pool.tile([P, 2, 2 * P], F32, name="tp", tag="ps")
                 for jj in range(2):
                     words = dwx[u][:, 2 * h + jj, :].bitcast(F32)
@@ -134,13 +159,9 @@ def tile_metalstmcell_pa_v_kernel(tc, src_x, zx, dx_w, w_x, d_x, grad_out, out_0
                 tps[u].append(tp)
 
         def evac_b(u):
-            grp_b[u] = work.tile([P, UNIT, J], BF16, name="grpb", tag="grpb", bufs=2, align_bytes=64)
-            gw = grp_b[u][:].bitcast(F32)
+            gw = grp_b[u].bitcast(F32)
             for h in range(2):
                 nc.scalar.copy(out=gw[:, h * 2 * P:(h + 1) * 2 * P, :], in_=tps[u][h][:].rearrange("q e r -> q r e"))
-
-        def quant_b(u):
-            cod_b[u], sca_b[u] = quant(grp_b[u], E5, "b", 2)
 
         def inter_w(u):
             grp_w[u] = work.tile([P, IN, J], BF16, name="grpw", tag="grpw", bufs=3, align_bytes=64)
@@ -154,7 +175,8 @@ def tile_metalstmcell_pa_v_kernel(tc, src_x, zx, dx_w, w_x, d_x, grad_out, out_0
 
         def mm1(u, r):
             ps1[(u, r)] = ps_pool.tile([P, IN], F32, name="ps1", tag="ps")
-            cols = slice(r * P, (r + 1) * P)
+            c0 = (r % R) * (UNIT // R) + (r // R) * P
+            cols = slice(c0, c0 + P)
             nc.tensor.matmul_mx(out=ps1[(u, r)][:], lhsT=cod_a[u][:, cols].bitcast(E5), lhsT_scale=sca_a[u][:, cols],
                                 rhs=src_codes[:].bitcast(E4), rhs_scale=src_scales[:], start=True, stop=True)
 
@@ -168,7 +190,7 @@ def tile_metalstmcell_pa_v_kernel(tc, src_x, zx, dx_w, w_x, d_x, grad_out, out_0
             else:
                 nc.scalar.copy(out=dst, in_=ps1[(u, r)][:])
             if r % 2 == 1:
-                nc.sync.dma_start(out=o1_v[:, u, r - 1:r + 1, :], in_=o1[u // 2][:, k - 1:k + 1, :])
+                nc.sync.dma_start(out=o1_v[:, u, r // 2], in_=o1[u // 2][:, k - 1:k + 1, :])
 
         def mm0(u):
             for j in range(J):
@@ -177,8 +199,9 @@ def tile_metalstmcell_pa_v_kernel(tc, src_x, zx, dx_w, w_x, d_x, grad_out, out_0
                                     rhs=cod_w[u][:].bitcast(E4), rhs_scale=sca_w[u][:], start=(u == 0), stop=(u == NU - 1))
 
         grp_s = work.tile([P, IN, J], BF16, name="grps", tag="grps", bufs=1, align_bytes=64)
-        mul(0)
-        transposes(0)
+        for hh in range(2):
+            mul_half(0, hh)
+            transposes(0, (hh,))
         inter_w(0)
         if S_IS:
             nc.scalar.copy(out=grp_s[:], in_=src_t[:].rearrange("p j i -> p i j"))
@@ -191,18 +214,16 @@ def tile_metalstmcell_pa_v_kernel(tc, src_x, zx, dx_w, w_x, d_x, grad_out, out_0
             if s == 0:
                 nc.vector.quantize_mx(out=src_codes[:].bitcast(E4), scales=src_scales[:], in_=grp_s[:].rearrange("p w j -> p (w j)"))
             if 1 <= s < NU:
-                quant_a(s - 1)
-                quant_b(s - 1)
+                quant_ab(s - 1)
             if s + 1 < NU:
                 mul(s + 1)
                 inter_w(s + 1)
             if s < NU:
-                evac_b(s)
                 inter_a(s, "s")
+                evac_b(s)
                 inter_a(s, "v")
             if s == NU - 1:
-                quant_a(s)
-                quant_b(s)
+                quant_ab(s)
             if s >= 1:
                 for r in range(4):
                     mm1(s - 1, r)

@@ -23,7 +23,6 @@ S_IW = []
 WIDE_DX = [2, 3]
 S_IS = False
 W_LEAD = 1
-R = 2
 V_EVAC = [(6, 2), (6, 3), (7, 1), (7, 3)]
 
 
@@ -34,7 +33,7 @@ def tile_metalstmcell_pa_v_kernel(tc, src_x, zx, dx_w, w_x, d_x, grad_out, out_0
     w_v = w_x.rearrange("g h i -> (g h) i").rearrange("(u p j) i -> p u (j i)", p=P, j=J)
     src_v = src_x.rearrange("(p j) i -> p j i", j=J)
     o0_v = out_0.rearrange("(p j) i -> p j i", j=J)
-    o1_v = out_1.rearrange("g h i -> (g h) i").rearrange("(u g m r) i -> m u g r i", u=NU, r=R, m=P)
+    o1_v = out_1.rearrange("g h i -> (g h) i").rearrange("(u r m) i -> m u r i", r=4, m=P)
 
     with ExitStack() as ctx:
         keep = ctx.enter_context(tc.tile_pool(name="keep", bufs=1))
@@ -126,13 +125,13 @@ def tile_metalstmcell_pa_v_kernel(tc, src_x, zx, dx_w, w_x, d_x, grad_out, out_0
                 grp_ab[u] = work.tile([P, 2, UNIT, J], BF16, name="grpab", tag="grpab", bufs=2, align_bytes=64)
                 grp_a[u] = grp_ab[u][:, 0]
                 grp_b[u] = grp_ab[u][:, 1]
-            ms = (UNIT - IA_V_COLS[u]) // R
-            dst = grp_a[u].rearrange("p (r m) j -> p r m j", r=R)
-            srcv = dwx[u][:].rearrange("p j (m r) -> p r m j", r=R)
+            split = UNIT - IA_V_COLS[u]
             if eng == "s":
-                nc.scalar.copy(out=dst[:, :, 0:ms, :], in_=srcv[:, :, 0:ms, :])
-            elif ms < UNIT // R:
-                nc.vector.tensor_copy(out=dst[:, :, ms:UNIT // R, :], in_=srcv[:, :, ms:UNIT // R, :])
+                nc.scalar.copy(out=grp_a[u][:, 0:split, :].rearrange("p (c i) t -> p c t i", i=4),
+                               in_=dwx[u][:, :, 0:split].rearrange("p t (c i) -> p c t i", i=4))
+            elif split < UNIT:
+                nc.vector.tensor_copy(out=grp_a[u][:, split:UNIT, :].rearrange("p (c i) t -> p c t i", i=4),
+                                      in_=dwx[u][:, :, split:UNIT].rearrange("p t (c i) -> p c t i", i=4))
 
         def quant(grp, fmt, tagc, bufs):
             codes = work.tile([P, UNIT], U32, name="c" + tagc, tag="c" + tagc, bufs=bufs, align_bytes=64)
@@ -168,15 +167,15 @@ def tile_metalstmcell_pa_v_kernel(tc, src_x, zx, dx_w, w_x, d_x, grad_out, out_0
             if u in S_IW:
                 nc.scalar.copy(out=grp_w[u][:], in_=w_of[u].rearrange("p j i -> p i j"))
             else:
-                nc.vector.tensor_copy(out=grp_w[u][:], in_=w_of[u].rearrange("p j i -> p i j"))
+                nc.vector.tensor_copy(out=grp_w[u][:].rearrange("p (c i) t -> p c t i", i=4),
+                                      in_=w_of[u].rearrange("p t (c i) -> p c t i", i=4))
 
         def quant_w(u):
             cod_w[u], sca_w[u] = quant(grp_w[u], E4, "w", W_LEAD + 2)
 
         def mm1(u, r):
             ps1[(u, r)] = ps_pool.tile([P, IN], F32, name="ps1", tag="ps")
-            c0 = (r % R) * (UNIT // R) + (r // R) * P
-            cols = slice(c0, c0 + P)
+            cols = slice(r * P, (r + 1) * P)
             nc.tensor.matmul_mx(out=ps1[(u, r)][:], lhsT=cod_a[u][:, cols].bitcast(E5), lhsT_scale=sca_a[u][:, cols],
                                 rhs=src_codes[:].bitcast(E4), rhs_scale=src_scales[:], start=True, stop=True)
 
@@ -190,7 +189,7 @@ def tile_metalstmcell_pa_v_kernel(tc, src_x, zx, dx_w, w_x, d_x, grad_out, out_0
             else:
                 nc.scalar.copy(out=dst, in_=ps1[(u, r)][:])
             if r % 2 == 1:
-                nc.sync.dma_start(out=o1_v[:, u, r // 2], in_=o1[u // 2][:, k - 1:k + 1, :])
+                nc.sync.dma_start(out=o1_v[:, u, r - 1:r + 1, :], in_=o1[u // 2][:, k - 1:k + 1, :])
 
         def mm0(u):
             for j in range(J):
@@ -206,7 +205,8 @@ def tile_metalstmcell_pa_v_kernel(tc, src_x, zx, dx_w, w_x, d_x, grad_out, out_0
         if S_IS:
             nc.scalar.copy(out=grp_s[:], in_=src_t[:].rearrange("p j i -> p i j"))
         else:
-            nc.vector.tensor_copy(out=grp_s[:], in_=src_t[:].rearrange("p j i -> p i j"))
+            nc.vector.tensor_copy(out=grp_s[:].rearrange("p (c i) t -> p c t i", i=4),
+                                  in_=src_t[:].rearrange("p t (c i) -> p c t i", i=4))
 
         for s in range(NU + 1):
             if s < NU:

@@ -18,12 +18,13 @@ P = 128
 J = 4
 UNIT = 512
 NU = GH // UNIT
-IA_V_COLS = [0, 0, 64, 64, 64, 64, 128, 320]
+IA_V_COLS = [0, 0, 32, 32, 32, 32, 64, 256]
 S_IW = []
 WIDE_DX = [2, 3]
 S_IS = False
 W_LEAD = 1
-V_EVAC = [(6, 2), (6, 3), (7, 1), (7, 3)]
+W_LAG = 1
+V_EVAC = [(7, 1), (7, 3)]
 
 
 def tile_metalstmcell_pa_v_kernel(tc, src_x, zx, dx_w, w_x, d_x, grad_out, out_0, out_1):
@@ -72,14 +73,19 @@ def tile_metalstmcell_pa_v_kernel(tc, src_x, zx, dx_w, w_x, d_x, grad_out, out_0
                 w_of[u0 + k] = w_t[:, k, :].rearrange("p (j i) -> p j i", j=J)
 
         src_t = keep.tile([P, J, IN], BF16, name="src", tag="src")
+        def load_wu(u):
+            w_t = keep.tile([P, J, IN], BF16, name="w%d" % u, tag="w%d" % u)
+            nc.sync.dma_start(out=w_t[:].rearrange("p j i -> p (j i)"), in_=w_v[:, u, :])
+            w_of[u] = w_t[:]
+
         for c in range(NU // 2):
             if c in WIDE_DX:
                 load_g(2 * c, 2)
                 load_dx(2 * c)
-                load_w(2 * c)
+                for u in (2 * c - W_LAG, 2 * c + 1 - W_LAG):
+                    load_wu(u)
             else:
                 dx_t = big.tile([P, 2, J, UNIT], F32, name="dx", tag="big")
-                w_t = keep.tile([P, 2, J * IN], BF16, name="w%d" % (2 * c), tag="w%d" % (2 * c))
                 for u in (2 * c, 2 * c + 1):
                     if u == 0:
                         g_t0 = keep.tile([P, J, UNIT], BF16, name="g0", tag="g0")
@@ -89,15 +95,17 @@ def tile_metalstmcell_pa_v_kernel(tc, src_x, zx, dx_w, w_x, d_x, grad_out, out_0
                             nc.sync.dma_start(out=dx_t[:, 0, js, :], in_=dx_v[:, js, 0:UNIT])
                         g_of[0] = g_t0[:]
                         dx_of[0] = dx_t[:, 0]
+                        nc.sync.dma_start(out=src_t[:], in_=src_v)
                     elif u == 1:
                         load_g(u, 1)
                     elif u == 2 * c:
                         load_g(u, 2)
                     if u > 0:
                         load_dx_unit(dx_t, u)
-                    load_w1(w_t, u)
-                    if u == 0:
-                        nc.sync.dma_start(out=src_t[:], in_=src_v)
+                    if u - W_LAG >= 0:
+                        load_wu(u - W_LAG)
+        for u in range(NU - W_LAG, NU):
+            load_wu(u)
 
         ident = keep.tile([P, P], F32, name="ident", tag="ident")
         make_identity(nc, ident[:])
@@ -201,24 +209,20 @@ def tile_metalstmcell_pa_v_kernel(tc, src_x, zx, dx_w, w_x, d_x, grad_out, out_0
         for hh in range(2):
             mul_half(0, hh)
             transposes(0, (hh,))
-        inter_w(0)
-        if S_IS:
-            nc.scalar.copy(out=grp_s[:], in_=src_t[:].rearrange("p j i -> p i j"))
-        else:
-            nc.vector.tensor_copy(out=grp_s[:].rearrange("p (c i) t -> p c t i", i=4),
-                                  in_=src_t[:].rearrange("p t (c i) -> p c t i", i=4))
+        nc.vector.tensor_copy(out=grp_s[:].rearrange("p (c i) t -> p c t i", i=4),
+                              in_=src_t[:].rearrange("p t (c i) -> p c t i", i=4))
 
         for s in range(NU + 1):
-            if s < NU:
-                quant_w(s)
+            if 1 <= s:
+                quant_w(s - 1)
             if s == 0:
                 nc.vector.quantize_mx(out=src_codes[:].bitcast(E4), scales=src_scales[:], in_=grp_s[:].rearrange("p w j -> p (w j)"))
             if 1 <= s < NU:
                 quant_ab(s - 1)
             if s + 1 < NU:
                 mul(s + 1)
-                inter_w(s + 1)
             if s < NU:
+                inter_w(s)
                 inter_a(s, "s")
                 evac_b(s)
                 inter_a(s, "v")

from contextlib import ExitStack

import concourse.mybir as mybir
from concourse.masks import make_identity

B, IN, GH = 512, 512, 4096
FLOPS = 2 * 2 * B * GH * IN
BYTES = 2 * B * IN + 2 * GH * IN + 4 * B * GH + 2 * B * GH + 4 * B * IN + 4 * GH * IN

F32 = mybir.dt.float32
BF16 = mybir.dt.bfloat16
U32 = mybir.dt.uint32
U8 = mybir.dt.uint8
E4 = mybir.dt.float8_e4m3fn_x4
E5 = mybir.dt.float8_e5m2_x4

P = 128
J = 4
UNIT = 512
NU = GH // UNIT
IA_V_COLS = [0, 0, 32, 32, 32, 32, 64, 256]
S_IW = []
WIDE_DX = [2, 3]
S_IS = False
W_LEAD = 1
W_LAG = 1
V_EVAC = [(7, 1), (7, 3)]


def tile_metalstmcell_pa_v_kernel(tc, src_x, zx, dx_w, w_x, d_x, grad_out, out_0, out_1):
    nc = tc.nc
    g_v = grad_out.rearrange("(p j) g h -> p j (g h)", j=J)
    dx_v = d_x.rearrange("(p j) g h -> p j (g h)", j=J)
    w_v = w_x.rearrange("g h i -> (g h) i").rearrange("(u p j) i -> p u (j i)", p=P, j=J)
    src_v = src_x.rearrange("(p j) i -> p j i", j=J)
    o0_v = out_0.rearrange("(p j) i -> p j i", j=J)
    o1_v = out_1.rearrange("g h i -> (g h) i").rearrange("(u r m) i -> m u r i", r=4, m=P)

    with ExitStack() as ctx:
        keep = ctx.enter_context(tc.tile_pool(name="keep", bufs=1))
        big = ctx.enter_context(tc.tile_pool(name="big", bufs=6))
        work = ctx.enter_context(tc.tile_pool(name="work", bufs=2))
        acc_pool = ctx.enter_context(tc.psum_pool(name="accp", bufs=1))
        ps_pool = ctx.enter_context(tc.psum_pool(name="psp", bufs=4))
        ctx.enter_context(tc.manual_schedule())

        g_of, dx_of, w_of = {}, {}, {}

        def load_g(u0, n):
            g_t = keep.tile([P, J, n * UNIT], BF16, name="g%d" % u0, tag="g%d" % u0)
            nc.sync.dma_start(out=g_t[:], in_=g_v[:, :, u0 * UNIT:(u0 + n) * UNIT])
            for k in range(n):
                g_of[u0 + k] = g_t[:, :, k * UNIT:(k + 1) * UNIT]

        def load_dx(u0):
            dx_t = big.tile([P, J, 2 * UNIT], F32, name="dx", tag="big")
            nc.sync.dma_start(out=dx_t[:], in_=dx_v[:, :, u0 * UNIT:(u0 + 2) * UNIT])
            for k in range(2):
                dx_of[u0 + k] = dx_t[:, :, k * UNIT:(k + 1) * UNIT]

        def load_dx_unit(dx_t, u):
            nc.sync.dma_start(out=dx_t[:, u % 2], in_=dx_v[:, :, u * UNIT:(u + 1) * UNIT])
            dx_of[u] = dx_t[:, u % 2]

        def load_w1(w_t, u):
            nc.sync.dma_start(out=w_t[:, u % 2, :], in_=w_v[:, u, :])
            w_of[u] = w_t[:, u % 2, :].rearrange("p (j i) -> p j i", j=J)

        def load_w(u0):
            w_t = keep.tile([P, 2, J * IN], BF16, name="w%d" % u0, tag="w%d" % u0)
            nc.sync.dma_start(out=w_t[:], in_=w_v[:, u0:u0 + 2, :])
            for k in range(2):
                w_of[u0 + k] = w_t[:, k, :].rearrange("p (j i) -> p j i", j=J)

        src_t = keep.tile([P, J, IN], BF16, name="src", tag="src")
        def load_wu(u):
            w_t = keep.tile([P, J, IN], BF16, name="w%d" % u, tag="w%d" % u)
            nc.sync.dma_start(out=w_t[:].rearrange("p j i -> p (j i)"), in_=w_v[:, u, :])
            w_of[u] = w_t[:]

        for c in range(NU // 2):
            if c in WIDE_DX:
                load_g(2 * c, 2)
                load_dx(2 * c)
                for u in (2 * c - W_LAG, 2 * c + 1 - W_LAG):
                    load_wu(u)
            else:
                dx_t = big.tile([P, 2, J, UNIT], F32, name="dx", tag="big")
                for u in (2 * c, 2 * c + 1):
                    if u == 0:
                        g_t0 = keep.tile([P, J, UNIT], BF16, name="g0", tag="g0")
                        for hh in range(2):
                            js = slice(2 * hh, 2 * hh + 2)
                            nc.sync.dma_start(out=g_t0[:, js, :], in_=g_v[:, js, 0:UNIT])
                            nc.sync.dma_start(out=dx_t[:, 0, js, :], in_=dx_v[:, js, 0:UNIT])
                        g_of[0] = g_t0[:]
                        dx_of[0] = dx_t[:, 0]
                        nc.sync.dma_start(out=src_t[:], in_=src_v)
                    elif u == 1:
                        load_g(u, 1)
                    elif u == 2 * c:
                        load_g(u, 2)
                    if u > 0:
                        load_dx_unit(dx_t, u)
                    if u - W_LAG >= 0:
                        load_wu(u - W_LAG)
        for u in range(NU - W_LAG, NU):
            load_wu(u)

        ident = keep.tile([P, P], F32, name="ident", tag="ident")
        make_identity(nc, ident[:])

        acc = [acc_pool.tile([P, IN], F32, name="acc%d" % j, tag="acc%d" % j) for j in range(J)]
        src_codes = keep.tile([P, IN], U32, name="srcc", tag="srcc", align_bytes=64)
        src_scales = keep.tile([P, IN], U8, name="srcs", tag="srcs", align_bytes=64)

        dwx, grp_a, grp_b, grp_w, grp_ab = {}, {}, {}, {}, {}
        cod_a, sca_a, cod_b, sca_b, cod_w, sca_w = {}, {}, {}, {}, {}, {}
        ps1, o1, tps = {}, {}, {}

        def mul(u):
            dwx[u] = work.tile([P, J, UNIT], BF16, name="dwx", tag="dwx", bufs=3)
            nc.vector.tensor_tensor(out=dwx[u][:], in0=g_of[u], in1=dx_of[u], op=mybir.AluOpType.mult)

        def mul_half(u, hh):
            if hh == 0:
                dwx[u] = work.tile([P, J, UNIT], BF16, name="dwx", tag="dwx", bufs=3)
            js = slice(2 * hh, 2 * hh + 2)
            nc.vector.tensor_tensor(out=dwx[u][:, js, :], in0=g_of[u][:, js, :], in1=dx_of[u][:, js, :], op=mybir.AluOpType.mult)

        def inter_a(u, eng):
            if u not in grp_a:
                grp_ab[u] = work.tile([P, 2, UNIT, J], BF16, name="grpab", tag="grpab", bufs=2, align_bytes=64)
                grp_a[u] = grp_ab[u][:, 0]
                grp_b[u] = grp_ab[u][:, 1]
            split = UNIT - IA_V_COLS[u]
            if eng == "s":
                nc.scalar.copy(out=grp_a[u][:, 0:split, :].rearrange("p (c i) t -> p c t i", i=4),
                               in_=dwx[u][:, :, 0:split].rearrange("p t (c i) -> p c t i", i=4))
            elif split < UNIT:
                nc.vector.tensor_copy(out=grp_a[u][:, split:UNIT, :].rearrange("p (c i) t -> p c t i", i=4),
                                      in_=dwx[u][:, :, split:UNIT].rearrange("p t (c i) -> p c t i", i=4))

        def quant(grp, fmt, tagc, bufs):
            codes = work.tile([P, UNIT], U32, name="c" + tagc, tag="c" + tagc, bufs=bufs, align_bytes=64)
            scales = work.tile([P, UNIT], U8, name="s" + tagc, tag="s" + tagc, bufs=bufs, align_bytes=64)
            nc.vector.quantize_mx(out=codes[:].bitcast(fmt), scales=scales[:], in_=grp[:].rearrange("p w j -> p (w j)"))
            return codes, scales

        def quant_ab(u):
            codes = work.tile([P, 2 * UNIT], U32, name="cab", tag="cab", bufs=2, align_bytes=64)
            scales = work.tile([P, 2 * UNIT], U8, name="sab", tag="sab", bufs=2, align_bytes=64)
            nc.vector.quantize_mx(out=codes[:].bitcast(E5), scales=scales[:], in_=grp_ab[u][:].rearrange("p a w j -> p (a w j)"))
            cod_a[u], sca_a[u] = codes[:, 0:UNIT], scales[:, 0:UNIT]
            cod_b[u], sca_b[u] = codes[:, UNIT:2 * UNIT], scales[:, UNIT:2 * UNIT]

        def transposes(u, banks=(0, 1)):
            if u not in tps:
                tps[u] = []
            for h in banks:
                tp = ps_pool.tile([P, 2, 2 * P], F32, name="tp", tag="ps")
                for jj in range(2):
                    words = dwx[u][:, 2 * h + jj, :].bitcast(F32)
                    for e in range(2):
                        nc.tensor.transpose(tp[:, e, jj * P:(jj + 1) * P], words[:, e:UNIT // 2:2], ident[:])
                tps[u].append(tp)

        def evac_b(u):
            gw = grp_b[u].bitcast(F32)
            for h in range(2):
                nc.scalar.copy(out=gw[:, h * 2 * P:(h + 1) * 2 * P, :], in_=tps[u][h][:].rearrange("q e r -> q r e"))

        def inter_w(u):
            grp_w[u] = work.tile([P, IN, J], BF16, name="grpw", tag="grpw", bufs=3, align_bytes=64)
            if u in S_IW:
                nc.scalar.copy(out=grp_w[u][:], in_=w_of[u].rearrange("p j i -> p i j"))
            else:
                nc.vector.tensor_copy(out=grp_w[u][:].rearrange("p (c i) t -> p c t i", i=4),
                                      in_=w_of[u].rearrange("p t (c i) -> p c t i", i=4))

        def quant_w(u):
            cod_w[u], sca_w[u] = quant(grp_w[u], E4, "w", W_LEAD + 2)

        def mm1(u, r):
            ps1[(u, r)] = ps_pool.tile([P, IN], F32, name="ps1", tag="ps")
            cols = slice(r * P, (r + 1) * P)
            nc.tensor.matmul_mx(out=ps1[(u, r)][:], lhsT=cod_a[u][:, cols].bitcast(E5), lhsT_scale=sca_a[u][:, cols],
                                rhs=src_codes[:].bitcast(E4), rhs_scale=src_scales[:], start=True, stop=True)

        def evac1(u, r):
            if u % 2 == 0 and r == 0:
                o1[u // 2] = big.tile([P, 8, IN], F32, name="o1", tag="big")
            k = (u % 2) * 4 + r
            dst = o1[u // 2][:, k, :]
            if (u, r) in V_EVAC:
                nc.vector.tensor_copy(out=dst, in_=ps1[(u, r)][:])
            else:
                nc.scalar.copy(out=dst, in_=ps1[(u, r)][:])
            if r % 2 == 1:
                nc.sync.dma_start(out=o1_v[:, u, r - 1:r + 1, :], in_=o1[u // 2][:, k - 1:k + 1, :])

        def mm0(u):
            for j in range(J):
                cols = slice(j * P, (j + 1) * P)
                nc.tensor.matmul_mx(out=acc[j][:], lhsT=cod_b[u][:, cols].bitcast(E5), lhsT_scale=sca_b[u][:, cols],
                                    rhs=cod_w[u][:].bitcast(E4), rhs_scale=sca_w[u][:], start=(u == 0), stop=(u == NU - 1))

        grp_s = work.tile([P, IN, J], BF16, name="grps", tag="grps", bufs=1, align_bytes=64)
        for hh in range(2):
            mul_half(0, hh)
            transposes(0, (hh,))
        nc.vector.tensor_copy(out=grp_s[:].rearrange("p (c i) t -> p c t i", i=4),
                              in_=src_t[:].rearrange("p t (c i) -> p c t i", i=4))

        for s in range(NU + 1):
            if 1 <= s:
                quant_w(s - 1)
            if s == 0:
                nc.vector.quantize_mx(out=src_codes[:].bitcast(E4), scales=src_scales[:], in_=grp_s[:].rearrange("p w j -> p (w j)"))
            if 1 <= s < NU:
                quant_ab(s - 1)
            if s + 1 < NU:
                mul(s + 1)
            if s < NU:
                inter_w(s)
                inter_a(s, "s")
                evac_b(s)
                inter_a(s, "v")
            if s == NU - 1:
                quant_ab(s)
            if s >= 1:
                for r in range(4):
                    mm1(s - 1, r)
                mm0(s - 1)
                for r in range(4):
                    evac1(s - 1, r)
            if s + 1 < NU:
                transposes(s + 1)

        o0 = big.tile([P, J, IN], F32, name="o0", tag="big")
        for h in range(2):
            nc.scalar.copy(out=o0[:, 2 * h, :], in_=acc[2 * h][:])
            nc.vector.tensor_copy(out=o0[:, 2 * h + 1, :], in_=acc[2 * h + 1][:])
            nc.sync.dma_start(out=o0_v[:, 2 * h:2 * h + 2, :], in_=o0[:, 2 * h:2 * h + 2, :])
